import numpy as np
import ml_dtypes


def mxq(x, axis, fmt="e4m3"):
    dtype, down = {"e4m3": (ml_dtypes.float8_e4m3fn, 7), "e5m2": (ml_dtypes.float8_e5m2, 14)}[fmt]
    v = np.moveaxis(np.asarray(x, np.float32).astype(ml_dtypes.bfloat16).astype(np.float64), axis, -1)
    blocks = v.reshape(v.shape[:-1] + (-1, 32))
    amax = np.abs(blocks).max(-1, keepdims=True)
    byte = np.maximum(np.where(amax > 0, np.frexp(amax)[1] - 1 + 127, 0) - down, 1)
    scale = np.exp2(byte - 127.0)
    codes = (blocks / scale).astype(np.float32).astype(dtype).astype(np.float64)
    return np.moveaxis((codes * scale).reshape(v.shape), -1, axis)


WIDE = False


def mx_kscale(k):
    if not WIDE:
        return np.ones(k)
    levels = np.array([10, -10, 5, -5, 0])
    if k % 512:
        return np.exp2(np.random.permutation(np.resize(levels, k // 32))).repeat(32)
    a = np.empty((k // 512, 16))
    for p in range(k // 512):
        a[p, :8] = np.random.permutation(np.resize(levels, 8))
        for g in range(8):
            far = levels[np.abs(levels - a[p, g]) >= 10]
            a[p, g + 8] = far[np.random.randint(len(far))]
    return np.exp2(a.ravel()).repeat(32)


BF16 = ml_dtypes.bfloat16


def bf(x):
    return np.asarray(x, np.float32).astype(BF16)


def f64(x):
    return np.asarray(x).astype(np.float64)


B, L, C, H, DH, AX = 2, 128, 8192, 16, 96, 3
D3 = DH // AX
HALF = D3 // 2
ROPE_BASE = 10000.0
COORD_MAX = 10.0


def rope_3d(x, coords):
    inv_freq = 1.0 / (ROPE_BASE ** (np.arange(HALF) / HALF))
    ang = coords[..., None] * inv_freq
    cos = np.cos(ang)[:, None]
    sin = np.sin(ang)[:, None]
    xr = x.reshape(B, H, L, AX, D3)
    x1, x2 = xr[..., :HALF], xr[..., HALF:]
    out = np.concatenate([x1 * cos - x2 * sin, x1 * sin + x2 * cos], axis=-1)
    return out.reshape(B, H, L, DH)


def setup_inputs():
    s = mx_kscale(C)
    return {"x_in": bf(np.random.standard_normal((B, L, C)) * s),
            "coords": bf(np.random.uniform(size=(B, L, AX)) * COORD_MAX),
            "w": bf(np.random.standard_normal((H * DH, C)) * 1.5 / np.sqrt(C) / s)}


def reference(x_in, coords, w):
    p = mxq(f64(x_in), 2, "e4m3") @ mxq(f64(w), 1, "e4m3").T
    p = p.reshape(B, L, H, DH).transpose(0, 2, 1, 3)
    return rope_3d(p, f64(coords))

@@ -1,0 +1,294 @@
+from contextlib import ExitStack
+import math
+
+import concourse.mybir as mybir
+from concourse.masks import make_identity
+
+F32 = mybir.dt.float32
+BF16 = mybir.dt.bfloat16
+U32 = mybir.dt.uint32
+U8 = mybir.dt.uint8
+FP8X4 = mybir.dt.float8_e4m3fn_x4
+ALU = mybir.AluOpType
+ACT = mybir.ActivationFunctionType
+
+P = 128
+BATCHES, TOKENS, K = 2, 128, 8192
+HEADS, HEAD_DIM, AXES, PAIRS = 16, 96, 3, 16
+FEATURES = HEADS * HEAD_DIM
+ROPE_BASE = 10000.0
+
+K_PASS = 512
+ROWS = 256
+ROW_TILES = ROWS // P
+PASSES_RUN = 8
+K_RUN = PASSES_RUN * K_PASS
+HALVES = K // K_RUN
+GROUPS = FEATURES // ROWS
+BANK = 512
+PAIR_WORDS = 2 * ROWS
+
+LOADS_RUN = 2
+PASSES_LOAD = PASSES_RUN // LOADS_RUN
+K_LOAD = PASSES_LOAD * K_PASS
+RUNS_AHEAD = 5
+TRANSPOSE_BANKS = 6
+VECTOR_EVERY = 3
+
+FLOPS = 2 * BATCHES * TOKENS * FEATURES * K
+
+ROUND_MAGIC = 1.5 * 2.0**23
+
+
+def leading_bits(value, bits):
+    scale = 1.0
+    while abs(value) * scale < 2.0 ** (bits - 1):
+        scale *= 2.0
+    while abs(value) * scale >= 2.0**bits:
+        scale /= 2.0
+    return round(value * scale) / scale
+
+
+def build_rotation_tables(nc, consts, coords_bf):
+    columns = BATCHES * AXES
+    shape = [P, columns, PAIRS]
+
+    freq_head = consts.tile([P, PAIRS], F32)
+    freq_tail = consts.tile([P, PAIRS], F32)
+    for i in range(PAIRS):
+        inv_freq = ROPE_BASE ** (-i / PAIRS)
+        head = leading_bits(inv_freq, 24)
+        nc.vector.memset(freq_head[:, i : i + 1], head)
+        nc.vector.memset(freq_tail[:, i : i + 1], inv_freq - head)
+
+    coords_f = consts.tile([P, columns], F32)
+    nc.vector.tensor_copy(out=coords_f[:], in_=coords_bf[:].rearrange("p b a -> p (b a)"))
+
+    coords_wide = coords_f[:].unsqueeze(2).to_broadcast(shape)
+    angle = consts.tile(shape, F32)
+    angle_tail = consts.tile(shape, F32)
+    nc.vector.tensor_tensor(
+        out=angle[:], in0=coords_wide, in1=freq_head[:].unsqueeze(1).to_broadcast(shape), op=ALU.mult
+    )
+    nc.vector.tensor_tensor(
+        out=angle_tail[:], in0=coords_wide, in1=freq_tail[:].unsqueeze(1).to_broadcast(shape), op=ALU.mult
+    )
+    nc.vector.tensor_tensor(out=angle[:], in0=angle[:], in1=angle_tail[:], op=ALU.add)
+
+    turns = consts.tile(shape, F32)
+    nc.vector.tensor_scalar(
+        out=turns[:], in0=angle[:], scalar1=1.0 / (2.0 * math.pi), scalar2=ROUND_MAGIC, op0=ALU.mult, op1=ALU.add
+    )
+    nc.vector.tensor_scalar(out=turns[:], in0=turns[:], scalar1=ROUND_MAGIC, scalar2=None, op0=ALU.subtract)
+
+    y = consts.tile(shape, F32)
+    part1 = leading_bits(2.0 * math.pi, 12)
+    part2 = leading_bits(2.0 * math.pi - part1, 12)
+    part3 = 2.0 * math.pi - part1 - part2
+    flat = "p c i -> p (c i)"
+    nc.vector.scalar_tensor_tensor(
+        out=y[:].rearrange(flat), in0=turns[:].rearrange(flat), scalar=-part1, in1=angle[:].rearrange(flat),
+        op0=ALU.mult, op1=ALU.add,
+    )
+    for part in (part2, part3):
+        nc.vector.scalar_tensor_tensor(
+            out=y[:].rearrange(flat), in0=turns[:].rearrange(flat), scalar=-part, in1=y[:].rearrange(flat),
+            op0=ALU.mult, op1=ALU.add,
+        )
+    pi_below = int(math.pi * 2.0**22) / 2.0**22
+    nc.vector.tensor_scalar(out=y[:], in0=y[:], scalar1=pi_below, scalar2=-pi_below, op0=ALU.min, op1=ALU.max)
+
+    z = consts.tile(shape, F32)
+    half_pi_head = leading_bits(math.pi / 2.0, 24)
+    nc.vector.scalar_tensor_tensor(
+        out=z[:].rearrange(flat), in0=y[:].rearrange(flat), scalar=-1.0, in1=y[:].rearrange(flat),
+        op0=ALU.mult, op1=ALU.max,
+    )
+    nc.vector.tensor_scalar(out=z[:], in0=z[:], scalar1=-1.0, scalar2=half_pi_head, op0=ALU.mult, op1=ALU.add)
+    nc.vector.tensor_scalar(out=z[:], in0=z[:], scalar1=math.pi / 2.0 - half_pi_head, scalar2=None, op0=ALU.add)
+    return y, z
+
+
+def tile_crossattnrope_pa_k_kernel(tc, x_in, coords, w, out):
+    nc = tc.nc
+    with ExitStack() as ctx:
+        consts = ctx.enter_context(tc.tile_pool(name="consts", bufs=1))
+        raw_pool = ctx.enter_context(tc.tile_pool(name="raw", bufs=(RUNS_AHEAD + 1) * LOADS_RUN))
+        grouped_pool = ctx.enter_context(tc.tile_pool(name="grouped", bufs=2))
+        w_mx_pool = ctx.enter_context(tc.tile_pool(name="w_mx", bufs=3))
+        rope_pool = ctx.enter_context(tc.tile_pool(name="rope", bufs=2))
+        bank_pool = ctx.enter_context(tc.psum_pool(name="banks", bufs=TRANSPOSE_BANKS))
+        sum_pool = ctx.enter_context(tc.psum_pool(name="sums", bufs=1))
+        ctx.enter_context(tc.manual_schedule())
+
+        x_rows = x_in.rearrange("b l k -> l b k")
+        runs = [("x", 0), (0, 0), ("x", 1), (0, 1)]
+        runs.extend((group, half) for group in range(1, GROUPS) for half in range(HALVES))
+
+        def load(run):
+            owner, half = run
+            pieces = []
+            for c in range(LOADS_RUN):
+                raw = raw_pool.tile([P, ROW_TILES * K_LOAD], BF16)
+                first_k = half * K_RUN + c * K_LOAD
+                k_cols = slice(first_k, first_k + K_LOAD)
+                if owner == "x":
+                    rows = x_rows[:, :, k_cols]
+                else:
+                    rows = w[owner * ROWS : (owner + 1) * ROWS, k_cols].rearrange("(j p) k -> p j k", p=P)
+                nc.sync.dma_start(out=raw[:].rearrange("p (j k) -> p j k", j=ROW_TILES), in_=rows)
+                pieces.append(raw)
+            return pieces
+
+        coords_bf = consts.tile([P, BATCHES, AXES], BF16)
+        nc.scalar.dma_start(out=coords_bf[:], in_=coords.rearrange("b l a -> l b a"))
+        raw_tiles = [load(run) for run in runs[:RUNS_AHEAD]]
+
+        zero = consts.tile([P, 1], F32)
+        nc.vector.memset(zero[:], 0.0)
+        warm = consts.tile([P, 1], F32)
+        nc.scalar.activation(out=warm[:], in_=zero[:], func=ACT.Sin)
+
+        identity = consts.tile([P, P], F32)
+        make_identity(nc, identity[:])
+
+        y, z = build_rotation_tables(nc, consts, coords_bf)
+        sin_table = consts.tile([P, BATCHES, AXES, PAIRS], F32)
+        minus_sin_table = consts.tile([P, BATCHES, AXES, PAIRS], F32)
+        cos_table = consts.tile([P, BATCHES, AXES, 2, PAIRS], F32)
+
+        x_codes = consts.tile([P, (K // K_PASS) * ROWS], U32, align_bytes=64)
+        x_scales = consts.tile([P, (K // K_PASS) * ROWS], U8, align_bytes=64)
+        product = consts.tile([P, BATCHES, FEATURES], F32)
+
+        def transpose_and_quantise(pieces, codes, scales):
+            grouped = grouped_pool.tile([P, PASSES_RUN * 4 * ROWS], BF16, align_bytes=64)
+            grouped_words = grouped[:].bitcast(F32)
+
+            def quantise_pair(first):
+                nc.vector.quantize_mx(
+                    out=codes[:, first * ROWS : first * ROWS + PAIR_WORDS].bitcast(FP8X4),
+                    scales=scales[:, first * ROWS : first * ROWS + PAIR_WORDS],
+                    in_=grouped[:, first * 4 * ROWS : (first + 2) * 4 * ROWS],
+                )
+
+            for g in range(PASSES_RUN):
+                bank = bank_pool.tile([P, BANK], F32)
+                raw_words = pieces[g // PASSES_LOAD][:].bitcast(F32)
+                for j in range(ROW_TILES):
+                    for u in range(2):
+                        first_word = j * (K_LOAD // 2) + (g % PASSES_LOAD) * (K_PASS // 2)
+                        piece = (j * 2 + u) * P
+                        nc.tensor.transpose(
+                            bank[:, piece : piece + P],
+                            raw_words[:, first_word + u : first_word + K_PASS // 2 : 2],
+                            identity[:],
+                        )
+                src = bank[:].rearrange("p (j u r) -> p j r u", j=ROW_TILES, u=2)
+                dst = grouped_words[:, g * BANK : (g + 1) * BANK].rearrange(
+                    "p (j r u) -> p j r u", j=ROW_TILES, u=2
+                )
+                if g % VECTOR_EVERY == VECTOR_EVERY - 1:
+                    nc.vector.tensor_copy(out=dst, in_=src)
+                else:
+                    nc.scalar.copy(out=dst, in_=src)
+                if g % 2 == 1 and g >= 3:
+                    quantise_pair(g - 3)
+            quantise_pair(PASSES_RUN - 2)
+
+        def multiply(half, codes, scales, sums):
+            for b in range(BATCHES):
+                for g in range(PASSES_RUN):
+                    x_first = ((half * PASSES_RUN + g) * BATCHES + b) * P
+                    nc.tensor.matmul_mx(
+                        out=sums[b][:],
+                        lhsT=x_codes[:, x_first : x_first + P].bitcast(FP8X4),
+                        lhsT_scale=x_scales[:, x_first : x_first + P],
+                        rhs=codes[:, g * ROWS : (g + 1) * ROWS].bitcast(FP8X4),
+                        rhs_scale=scales[:, g * ROWS : (g + 1) * ROWS],
+                        start=(half == 0 and g == 0),
+                        stop=(half == HALVES - 1 and g == PASSES_RUN - 1),
+                    )
+
+        def rotate_and_store(first_head, end_head, first_batch, end_batch, queue):
+            n = end_head - first_head
+            bs = slice(first_batch, end_batch)
+            nb = end_batch - first_batch
+            heads = product[:].rearrange("p b (h f) -> p b h f", f=HEAD_DIM)[:, bs, first_head:end_head, :]
+            halves = product[:].rearrange("p b (h a s i) -> p b h a s i", a=AXES, s=2, i=PAIRS)
+            halves = halves[:, bs, first_head:end_head]
+            rotated = rope_pool.tile([P, BATCHES, 3, HEAD_DIM], F32)
+            crossed = rope_pool.tile([P, BATCHES, 3, HEAD_DIM], F32)
+            crossed_halves = crossed[:].rearrange("p b h (a s i) -> p b h a s i", a=AXES, s=2)[:, bs, :n]
+            pair_shape = [P, nb, n, AXES, PAIRS]
+            nc.vector.tensor_tensor(
+                out=rotated[:, bs, :n, :],
+                in0=heads,
+                in1=cos_table[:, bs].rearrange("p b a s i -> p b (a s i)").unsqueeze(2).to_broadcast(
+                    [P, nb, n, HEAD_DIM]
+                ),
+                op=ALU.mult,
+            )
+            nc.vector.tensor_tensor(
+                out=crossed_halves[:, :, :, :, 0, :],
+                in0=halves[:, :, :, :, 1, :],
+                in1=minus_sin_table[:, bs].unsqueeze(2).to_broadcast(pair_shape),
+                op=ALU.mult,
+            )
+            nc.vector.tensor_tensor(
+                out=crossed_halves[:, :, :, :, 1, :],
+                in0=halves[:, :, :, :, 0, :],
+                in1=sin_table[:, bs].unsqueeze(2).to_broadcast(pair_shape),
+                op=ALU.mult,
+            )
+            nc.vector.tensor_tensor(
+                out=rotated[:, bs, :n, :], in0=rotated[:, bs, :n, :], in1=crossed[:, bs, :n, :], op=ALU.add
+            )
+            for b in range(first_batch, end_batch):
+                queue.dma_start(
+                    out=out[b, first_head:end_head].rearrange("h l d -> l h d"), in_=rotated[:, b, :n, :]
+                )
+
+        waiting = None
+        sums = None
+        for r, run in enumerate(runs):
+            owner, half = run
+            if r + RUNS_AHEAD < len(runs):
+                raw_tiles.append(load(runs[r + RUNS_AHEAD]))
+            if owner == "x":
+                first = half * PASSES_RUN * ROWS
+                codes = x_codes[:, first : first + PASSES_RUN * ROWS]
+                scales = x_scales[:, first : first + PASSES_RUN * ROWS]
+            else:
+                w_codes = w_mx_pool.tile([P, PASSES_RUN * ROWS], U32, align_bytes=64)
+                w_scales = w_mx_pool.tile([P, PASSES_RUN * ROWS], U8, align_bytes=64)
+                codes, scales = w_codes[:], w_scales[:]
+            transpose_and_quantise(raw_tiles[r], codes, scales)
+
+            if r == 0:
+                flat = "p b a i -> p (b a) i"
+                nc.scalar.activation(out=sin_table[:].rearrange(flat), in_=y[:], func=ACT.Sin)
+                nc.scalar.activation(out=minus_sin_table[:].rearrange(flat), in_=y[:], func=ACT.Sin, scale=-1.0)
+                for s in range(2):
+                    nc.scalar.activation(out=cos_table[:, :, :, s, :].rearrange(flat), in_=z[:], func=ACT.Sin)
+
+            last = r == len(runs) - 1
+            for todo in ([waiting] if not last else [waiting, (owner, half, codes, scales)]):
+                if todo is None:
+                    continue
+                group, group_half, group_codes, group_scales = todo
+                if group_half == 0:
+                    sums = [
+                        sum_pool.tile([P, ROWS], F32, name="sum%d" % b, tag="sum%d" % b) for b in range(BATCHES)
+                    ]
+                multiply(group_half, group_codes, group_scales, sums)
+                if group_half == HALVES - 1:
+                    for b in range(BATCHES):
+                        nc.scalar.copy(out=product[:, b, group * ROWS : (group + 1) * ROWS], in_=sums[b][:])
+                    first_head, end_head = group * ROWS // HEAD_DIM, (group + 1) * ROWS // HEAD_DIM
+                    if group < GROUPS - 1:
+                        rotate_and_store(first_head, end_head, 0, BATCHES, nc.gpsimd)
+                    else:
+                        for b in range(BATCHES):
+                            rotate_and_store(first_head, end_head, b, b + 1, nc.sync)
+            waiting = None if owner == "x" else (owner, half, codes, scales)

@@ -19,21 +19,27 @@ FEATURES = HEADS * HEAD_DIM
 ROPE_BASE = 10000.0
 
 K_PASS = 512
+PASS_WORDS = K_PASS // 2
 ROWS = 256
 ROW_TILES = ROWS // P
-PASSES_RUN = 8
-K_RUN = PASSES_RUN * K_PASS
-HALVES = K // K_RUN
+PASSES_UNIT = 4
+K_UNIT = PASSES_UNIT * K_PASS
+QUARTERS = K // K_UNIT
 GROUPS = FEATURES // ROWS
 BANK = 512
+UNIT_WORDS = PASSES_UNIT * ROWS
 PAIR_WORDS = 2 * ROWS
 
-LOADS_RUN = 2
-PASSES_LOAD = PASSES_RUN // LOADS_RUN
-K_LOAD = PASSES_LOAD * K_PASS
-RUNS_AHEAD = 5
+BLOCK = 2 * PAIRS
+BLOCKS_GROUP = ROWS // BLOCK
+TABLE_BLOCKS = BLOCKS_GROUP + AXES - 1
+
+UNITS_AHEAD = 10
+REORDER_AHEAD = 2
+MX_LAG = 2
 TRANSPOSE_BANKS = 6
-VECTOR_EVERY = 3
+SPLIT_QUARTERS = (3,)
+VECTOR_BANKS = ()
 
 FLOPS = 2 * BATCHES * TOKENS * FEATURES * K
 
@@ -49,17 +55,20 @@ def leading_bits(value, bits):
     return round(value * scale) / scale
 
 
-def build_rotation_tables(nc, consts, coords_bf):
-    columns = BATCHES * AXES
-    shape = [P, columns, PAIRS]
-
+def build_frequencies(nc, consts):
     freq_head = consts.tile([P, PAIRS], F32)
     freq_tail = consts.tile([P, PAIRS], F32)
     for i in range(PAIRS):
         inv_freq = ROPE_BASE ** (-i / PAIRS)
         head = leading_bits(inv_freq, 24)
-        nc.vector.memset(freq_head[:, i : i + 1], head)
-        nc.vector.memset(freq_tail[:, i : i + 1], inv_freq - head)
+        nc.gpsimd.memset(freq_head[:, i : i + 1], head)
+        nc.gpsimd.memset(freq_tail[:, i : i + 1], inv_freq - head)
+    return freq_head, freq_tail
+
+
+def build_angles(nc, consts, coords_bf, freq_head, freq_tail):
+    columns = BATCHES * AXES
+    shape = [P, columns, PAIRS]
 
     coords_f = consts.tile([P, columns], F32)
     nc.vector.tensor_copy(out=coords_f[:], in_=coords_bf[:].rearrange("p b a -> p (b a)"))
@@ -113,36 +122,47 @@ def tile_crossattnrope_pa_k_kernel(tc, x_in, coords, w, out):
     nc = tc.nc
     with ExitStack() as ctx:
         consts = ctx.enter_context(tc.tile_pool(name="consts", bufs=1))
-        raw_pool = ctx.enter_context(tc.tile_pool(name="raw", bufs=(RUNS_AHEAD + 1) * LOADS_RUN))
-        grouped_pool = ctx.enter_context(tc.tile_pool(name="grouped", bufs=2))
-        w_mx_pool = ctx.enter_context(tc.tile_pool(name="w_mx", bufs=3))
+        raw_pool = ctx.enter_context(tc.tile_pool(name="raw", bufs=UNITS_AHEAD + 2))
+        ordered_pool = ctx.enter_context(tc.tile_pool(name="ordered", bufs=REORDER_AHEAD + 1))
+        grouped_pool = ctx.enter_context(tc.tile_pool(name="grouped", bufs=3))
+        w_mx_pool = ctx.enter_context(tc.tile_pool(name="w_mx", bufs=QUARTERS + MX_LAG + 2))
         rope_pool = ctx.enter_context(tc.tile_pool(name="rope", bufs=2))
         bank_pool = ctx.enter_context(tc.psum_pool(name="banks", bufs=TRANSPOSE_BANKS))
-        sum_pool = ctx.enter_context(tc.psum_pool(name="sums", bufs=1))
+        sum_pool = ctx.enter_context(tc.psum_pool(name="sums", bufs=2))
         ctx.enter_context(tc.manual_schedule())
 
         x_rows = x_in.rearrange("b l k -> l b k")
-        runs = [("x", 0), (0, 0), ("x", 1), (0, 1)]
-        runs.extend((group, half) for group in range(1, GROUPS) for half in range(HALVES))
+        units = []
+        for quarter in range(QUARTERS):
+            units.extend([("x", quarter), (0, quarter)])
+        units.extend((group, quarter) for group in range(1, GROUPS) for quarter in range(QUARTERS))
+        last_unit = len(units) - 1
 
-        def load(run):
-            owner, half = run
-            pieces = []
-            for c in range(LOADS_RUN):
-                raw = raw_pool.tile([P, ROW_TILES * K_LOAD], BF16)
-                first_k = half * K_RUN + c * K_LOAD
-                k_cols = slice(first_k, first_k + K_LOAD)
+        raw_tiles = []
+
+        def load(n):
+            if n > last_unit:
+                return
+            owner, quarter = units[n]
+            raw = raw_pool.tile([P, ROW_TILES * K_UNIT], BF16)
+            pieces = PASSES_UNIT if n == 0 else 1
+            width = K_UNIT // pieces
+            for c in range(pieces):
+                first_k = quarter * K_UNIT + c * width
+                k_cols = slice(first_k, first_k + width)
                 if owner == "x":
                     rows = x_rows[:, :, k_cols]
                 else:
                     rows = w[owner * ROWS : (owner + 1) * ROWS, k_cols].rearrange("(j p) k -> p j k", p=P)
-                nc.sync.dma_start(out=raw[:].rearrange("p (j k) -> p j k", j=ROW_TILES), in_=rows)
-                pieces.append(raw)
-            return pieces
+                nc.sync.dma_start(
+                    out=raw[:].rearrange("p (j k) -> p j k", j=ROW_TILES)[:, :, c * width : (c + 1) * width], in_=rows
+                )
+            raw_tiles.append(raw)
 
         coords_bf = consts.tile([P, BATCHES, AXES], BF16)
         nc.scalar.dma_start(out=coords_bf[:], in_=coords.rearrange("b l a -> l b a"))
-        raw_tiles = [load(run) for run in runs[:RUNS_AHEAD]]
+        for n in range(UNITS_AHEAD):
+            load(n)
 
         zero = consts.tile([P, 1], F32)
         nc.vector.memset(zero[:], 0.0)
@@ -151,144 +171,165 @@ def tile_crossattnrope_pa_k_kernel(tc, x_in, coords, w, out):
 
         identity = consts.tile([P, P], F32)
         make_identity(nc, identity[:])
+        freq_head, freq_tail = build_frequencies(nc, consts)
 
-        y, z = build_rotation_tables(nc, consts, coords_bf)
-        sin_table = consts.tile([P, BATCHES, AXES, PAIRS], F32)
-        minus_sin_table = consts.tile([P, BATCHES, AXES, PAIRS], F32)
-        cos_table = consts.tile([P, BATCHES, AXES, 2, PAIRS], F32)
+        cos_table = consts.tile([P, BATCHES, TABLE_BLOCKS, 2, PAIRS], F32)
+        sin_table = consts.tile([P, BATCHES, TABLE_BLOCKS, 2, PAIRS], F32)
 
-        x_codes = consts.tile([P, (K // K_PASS) * ROWS], U32, align_bytes=64)
-        x_scales = consts.tile([P, (K // K_PASS) * ROWS], U8, align_bytes=64)
-        product = consts.tile([P, BATCHES, FEATURES], F32)
+        x_codes = consts.tile([P, QUARTERS * UNIT_WORDS], U32, align_bytes=64)
+        x_scales = consts.tile([P, QUARTERS * UNIT_WORDS], U8, align_bytes=64)
+        rotated = consts.tile([P, BATCHES, FEATURES], F32)
 
-        def transpose_and_quantise(pieces, codes, scales):
-            grouped = grouped_pool.tile([P, PASSES_RUN * 4 * ROWS], BF16, align_bytes=64)
+        def fill_tables(y, z):
+            y_axes = y[:].rearrange("p (b a) i -> p b a i", b=BATCHES)
+            z_axes = z[:].rearrange("p (b a) i -> p b a i", b=BATCHES)
+            for s in range(2):
+                for first in range(0, TABLE_BLOCKS, AXES):
+                    n = min(AXES, TABLE_BLOCKS - first)
+                    nc.scalar.activation(
+                        out=sin_table[:, :, first : first + n, s, :], in_=y_axes[:, :, :n, :], func=ACT.Sin,
+                        scale=(-1.0 if s == 0 else 1.0),
+                    )
+                    nc.scalar.activation(
+                        out=cos_table[:, :, first : first + n, s, :], in_=z_axes[:, :, :n, :], func=ACT.Sin
+                    )
+
+        ordered_tiles = {}
+
+        def reorder(n):
+            if n > last_unit or units[n][0] == "x":
+                return
+            ordered = ordered_pool.tile([P, ROW_TILES * K_UNIT], BF16)
+            src = raw_tiles[n][:].bitcast(F32).rearrange("q (n p u) -> q n u p", u=2, p=P)
+            dst = ordered[:].bitcast(F32).rearrange("q (n u p) -> q n u p", u=2, p=P)
+            if units[n][1] in SPLIT_QUARTERS:
+                nc.vector.tensor_copy(out=dst[:, :PASSES_UNIT], in_=src[:, :PASSES_UNIT])
+                nc.scalar.copy(out=dst[:, PASSES_UNIT:], in_=src[:, PASSES_UNIT:])
+            else:
+                nc.vector.tensor_copy(out=dst, in_=src)
+            ordered_tiles[n] = ordered
+
+        grouped_tiles = {}
+
+        def transpose(n):
+            grouped = grouped_pool.tile([P, PASSES_UNIT * 4 * ROWS], BF16, align_bytes=64)
+            grouped_tiles[n] = grouped
             grouped_words = grouped[:].bitcast(F32)
-
-            def quantise_pair(first):
-                nc.vector.quantize_mx(
-                    out=codes[:, first * ROWS : first * ROWS + PAIR_WORDS].bitcast(FP8X4),
-                    scales=scales[:, first * ROWS : first * ROWS + PAIR_WORDS],
-                    in_=grouped[:, first * 4 * ROWS : (first + 2) * 4 * ROWS],
-                )
-
-            for g in range(PASSES_RUN):
+            for g in range(PASSES_UNIT):
                 bank = bank_pool.tile([P, BANK], F32)
-                raw_words = pieces[g // PASSES_LOAD][:].bitcast(F32)
                 for j in range(ROW_TILES):
+                    first_word = (j * PASSES_UNIT + g) * PASS_WORDS
                     for u in range(2):
-                        first_word = j * (K_LOAD // 2) + (g % PASSES_LOAD) * (K_PASS // 2)
-                        piece = (j * 2 + u) * P
-                        nc.tensor.transpose(
-                            bank[:, piece : piece + P],
-                            raw_words[:, first_word + u : first_word + K_PASS // 2 : 2],
-                            identity[:],
-                        )
+                        if n in ordered_tiles:
+                            words = ordered_tiles[n][:].bitcast(F32)
+                            piece = words[:, first_word + u * P : first_word + (u + 1) * P]
+                        else:
+                            words = raw_tiles[n][:].bitcast(F32)
+                            piece = words[:, first_word + u : first_word + PASS_WORDS : 2]
+                        column = (j * 2 + u) * P
+                        nc.tensor.transpose(bank[:, column : column + P], piece, identity[:])
                 src = bank[:].rearrange("p (j u r) -> p j r u", j=ROW_TILES, u=2)
                 dst = grouped_words[:, g * BANK : (g + 1) * BANK].rearrange(
                     "p (j r u) -> p j r u", j=ROW_TILES, u=2
                 )
-                if g % VECTOR_EVERY == VECTOR_EVERY - 1:
+                if (n, g) in VECTOR_BANKS:
                     nc.vector.tensor_copy(out=dst, in_=src)
                 else:
                     nc.scalar.copy(out=dst, in_=src)
-                if g % 2 == 1 and g >= 3:
-                    quantise_pair(g - 3)
-            quantise_pair(PASSES_RUN - 2)
 
-        def multiply(half, codes, scales, sums):
-            for b in range(BATCHES):
-                for g in range(PASSES_RUN):
-                    x_first = ((half * PASSES_RUN + g) * BATCHES + b) * P
+        mx_tiles = {}
+
+        def quantise(n):
+            owner, quarter = units[n]
+            if owner == "x":
+                codes = x_codes[:, quarter * UNIT_WORDS : (quarter + 1) * UNIT_WORDS]
+                scales = x_scales[:, quarter * UNIT_WORDS : (quarter + 1) * UNIT_WORDS]
+            else:
+                w_codes = w_mx_pool.tile([P, UNIT_WORDS], U32, align_bytes=64)
+                w_scales = w_mx_pool.tile([P, UNIT_WORDS], U8, align_bytes=64)
+                codes, scales = w_codes[:], w_scales[:]
+                mx_tiles[(owner, quarter)] = (codes, scales)
+            for first in range(0, UNIT_WORDS, PAIR_WORDS):
+                nc.vector.quantize_mx(
+                    out=codes[:, first : first + PAIR_WORDS].bitcast(FP8X4),
+                    scales=scales[:, first : first + PAIR_WORDS],
+                    in_=grouped_tiles[n][:, 4 * first : 4 * (first + PAIR_WORDS)],
+                )
+
+        sums = {}
+
+        def multiply(group, b, quarters):
+            if quarters[0] == 0:
+                total = sum_pool.tile([P, ROWS], F32)
+                sums[(group, b)] = total
+            for quarter in quarters:
+                codes, scales = mx_tiles[(group, quarter)]
+                for g in range(PASSES_UNIT):
+                    x_first = ((quarter * PASSES_UNIT + g) * BATCHES + b) * P
                     nc.tensor.matmul_mx(
-                        out=sums[b][:],
+                        out=sums[(group, b)][:],
                         lhsT=x_codes[:, x_first : x_first + P].bitcast(FP8X4),
                         lhsT_scale=x_scales[:, x_first : x_first + P],
                         rhs=codes[:, g * ROWS : (g + 1) * ROWS].bitcast(FP8X4),
                         rhs_scale=scales[:, g * ROWS : (g + 1) * ROWS],
-                        start=(half == 0 and g == 0),
-                        stop=(half == HALVES - 1 and g == PASSES_RUN - 1),
+                        start=(quarter == 0 and g == 0),
+                        stop=(quarter == QUARTERS - 1 and g == PASSES_UNIT - 1),
                     )
 
-        def rotate_and_store(first_head, end_head, first_batch, end_batch, queue):
-            n = end_head - first_head
-            bs = slice(first_batch, end_batch)
-            nb = end_batch - first_batch
-            heads = product[:].rearrange("p b (h f) -> p b h f", f=HEAD_DIM)[:, bs, first_head:end_head, :]
-            halves = product[:].rearrange("p b (h a s i) -> p b h a s i", a=AXES, s=2, i=PAIRS)
-            halves = halves[:, bs, first_head:end_head]
-            rotated = rope_pool.tile([P, BATCHES, 3, HEAD_DIM], F32)
-            crossed = rope_pool.tile([P, BATCHES, 3, HEAD_DIM], F32)
-            crossed_halves = crossed[:].rearrange("p b h (a s i) -> p b h a s i", a=AXES, s=2)[:, bs, :n]
-            pair_shape = [P, nb, n, AXES, PAIRS]
+        def rotate_and_store(group, b):
+            cols = slice(group * ROWS, (group + 1) * ROWS)
+            axis = group * BLOCKS_GROUP % AXES
+            blocks = slice(axis, axis + BLOCKS_GROUP)
+            total = sums[(group, b)]
+            turned = rotated[:, b, cols]
+            crossed = rope_pool.tile([P, ROWS], F32)
+            halves = "p (c s i) -> p c s i"
             nc.vector.tensor_tensor(
-                out=rotated[:, bs, :n, :],
-                in0=heads,
-                in1=cos_table[:, bs].rearrange("p b a s i -> p b (a s i)").unsqueeze(2).to_broadcast(
-                    [P, nb, n, HEAD_DIM]
+                out=turned, in0=total[:], in1=cos_table[:, b, blocks].rearrange("p c s i -> p (c s i)"), op=ALU.mult
+            )
+            nc.vector.tensor_tensor(
+                out=crossed[:].rearrange(halves, s=2, i=PAIRS),
+                in0=total[:].rearrange(halves, s=2, i=PAIRS)[:, :, ::-1, :],
+                in1=sin_table[:, b, blocks],
+                op=ALU.mult,
+            )
+            nc.vector.tensor_tensor(out=turned, in0=turned, in1=crossed[:], op=ALU.add)
+            first_head, end_head = group * ROWS // HEAD_DIM, (group + 1) * ROWS // HEAD_DIM
+            nc.sync.dma_start(
+                out=out[b, first_head:end_head].rearrange("h l d -> l h d"),
+                in_=rotated[:, b, first_head * HEAD_DIM : end_head * HEAD_DIM].rearrange(
+                    "p (h d) -> p h d", d=HEAD_DIM
                 ),
-                op=ALU.mult,
             )
-            nc.vector.tensor_tensor(
-                out=crossed_halves[:, :, :, :, 0, :],
-                in0=halves[:, :, :, :, 1, :],
-                in1=minus_sin_table[:, bs].unsqueeze(2).to_broadcast(pair_shape),
-                op=ALU.mult,
-            )
-            nc.vector.tensor_tensor(
-                out=crossed_halves[:, :, :, :, 1, :],
-                in0=halves[:, :, :, :, 0, :],
-                in1=sin_table[:, bs].unsqueeze(2).to_broadcast(pair_shape),
-                op=ALU.mult,
-            )
-            nc.vector.tensor_tensor(
-                out=rotated[:, bs, :n, :], in0=rotated[:, bs, :n, :], in1=crossed[:, bs, :n, :], op=ALU.add
-            )
-            for b in range(first_batch, end_batch):
-                queue.dma_start(
-                    out=out[b, first_head:end_head].rearrange("h l d -> l h d"), in_=rotated[:, b, :n, :]
-                )
 
-        waiting = None
-        sums = None
-        for r, run in enumerate(runs):
-            owner, half = run
-            if r + RUNS_AHEAD < len(runs):
-                raw_tiles.append(load(runs[r + RUNS_AHEAD]))
-            if owner == "x":
-                first = half * PASSES_RUN * ROWS
-                codes = x_codes[:, first : first + PASSES_RUN * ROWS]
-                scales = x_scales[:, first : first + PASSES_RUN * ROWS]
-            else:
-                w_codes = w_mx_pool.tile([P, PASSES_RUN * ROWS], U32, align_bytes=64)
-                w_scales = w_mx_pool.tile([P, PASSES_RUN * ROWS], U8, align_bytes=64)
-                codes, scales = w_codes[:], w_scales[:]
-            transpose_and_quantise(raw_tiles[r], codes, scales)
+        after_transposes = {}
+        for group in range(GROUPS - 1):
+            done = units.index((group, QUARTERS - 1))
+            for b in range(BATCHES):
+                after_transposes.setdefault(done + MX_LAG + b, []).append((group, b))
 
-            if r == 0:
-                flat = "p b a i -> p (b a) i"
-                nc.scalar.activation(out=sin_table[:].rearrange(flat), in_=y[:], func=ACT.Sin)
-                nc.scalar.activation(out=minus_sin_table[:].rearrange(flat), in_=y[:], func=ACT.Sin, scale=-1.0)
-                for s in range(2):
-                    nc.scalar.activation(out=cos_table[:, :, :, s, :].rearrange(flat), in_=z[:], func=ACT.Sin)
+        y, z = build_angles(nc, consts, coords_bf, freq_head, freq_tail)
+        for n in range(REORDER_AHEAD):
+            reorder(n)
+        for n in range(last_unit + 1):
+            load(n + UNITS_AHEAD)
+            reorder(n + REORDER_AHEAD)
+            transpose(n)
+            for group, b in after_transposes.get(n, []):
+                multiply(group, b, range(QUARTERS))
+            if n > 0:
+                quantise(n - 1)
+            if n == 4:
+                fill_tables(y, z)
+            for group, b in after_transposes.get(n - 1, []):
+                rotate_and_store(group, b)
 
-            last = r == len(runs) - 1
-            for todo in ([waiting] if not last else [waiting, (owner, half, codes, scales)]):
-                if todo is None:
-                    continue
-                group, group_half, group_codes, group_scales = todo
-                if group_half == 0:
-                    sums = [
-                        sum_pool.tile([P, ROWS], F32, name="sum%d" % b, tag="sum%d" % b) for b in range(BATCHES)
-                    ]
-                multiply(group_half, group_codes, group_scales, sums)
-                if group_half == HALVES - 1:
-                    for b in range(BATCHES):
-                        nc.scalar.copy(out=product[:, b, group * ROWS : (group + 1) * ROWS], in_=sums[b][:])
-                    first_head, end_head = group * ROWS // HEAD_DIM, (group + 1) * ROWS // HEAD_DIM
-                    if group < GROUPS - 1:
-                        rotate_and_store(first_head, end_head, 0, BATCHES, nc.gpsimd)
-                    else:
-                        for b in range(BATCHES):
-                            rotate_and_store(first_head, end_head, b, b + 1, nc.sync)
-            waiting = None if owner == "x" else (owner, half, codes, scales)
+        last_group = GROUPS - 1
+        for group, b in after_transposes.get(last_unit, []):
+            rotate_and_store(group, b)
+        for b in range(BATCHES):
+            multiply(last_group, b, range(QUARTERS - 1))
+        quantise(last_unit)
+        for b in range(BATCHES):
+            multiply(last_group, b, range(QUARTERS - 1, QUARTERS))
+            rotate_and_store(last_group, b)

@@ -302,11 +302,18 @@ def tile_crossattnrope_pa_k_kernel(tc, x_in, coords, w, out):
                 ),
             )
 
-        after_transposes = {}
-        for group in range(GROUPS - 1):
-            done = units.index((group, QUARTERS - 1))
+        def multiply_unit(n):
+            if n < 0 or units[n][0] == "x":
+                return
+            group, quarter = units[n]
             for b in range(BATCHES):
-                after_transposes.setdefault(done + MX_LAG + b, []).append((group, b))
+                multiply(group, b, (quarter,))
+
+        def finish_group(n):
+            if n < 0 or units[n][0] == "x" or units[n][1] < QUARTERS - 1:
+                return
+            for b in range(BATCHES):
+                rotate_and_store(units[n][0], b)
 
         y, z = build_angles(nc, consts, coords_bf, freq_head, freq_tail)
         for n in range(REORDER_AHEAD):
@@ -315,21 +322,15 @@ def tile_crossattnrope_pa_k_kernel(tc, x_in, coords, w, out):
             load(n + UNITS_AHEAD)
             reorder(n + REORDER_AHEAD)
             transpose(n)
-            for group, b in after_transposes.get(n, []):
-                multiply(group, b, range(QUARTERS))
+            multiply_unit(n - MX_LAG)
+            finish_group(n - MX_LAG - 1)
             if n > 0:
                 quantise(n - 1)
             if n == 4:
                 fill_tables(y, z)
-            for group, b in after_transposes.get(n - 1, []):
-                rotate_and_store(group, b)
 
-        last_group = GROUPS - 1
-        for group, b in after_transposes.get(last_unit, []):
-            rotate_and_store(group, b)
-        for b in range(BATCHES):
-            multiply(last_group, b, range(QUARTERS - 1))
+        multiply_unit(last_unit - 1)
         quantise(last_unit)
         for b in range(BATCHES):
-            multiply(last_group, b, range(QUARTERS - 1, QUARTERS))
-            rotate_and_store(last_group, b)
+            multiply(GROUPS - 1, b, (QUARTERS - 1,))
+            rotate_and_store(GROUPS - 1, b)

@@ -36,10 +36,9 @@ TABLE_BLOCKS = BLOCKS_GROUP + AXES - 1
 
 UNITS_AHEAD = 10
 REORDER_AHEAD = 2
-MX_LAG = 2
+MX_LAG = 3
 TRANSPOSE_BANKS = 6
-SPLIT_QUARTERS = (3,)
-VECTOR_BANKS = ()
+STRIDED_QUARTERS = (3,)
 
 FLOPS = 2 * BATCHES * TOKENS * FEATURES * K
 
@@ -122,10 +121,10 @@ def tile_crossattnrope_pa_k_kernel(tc, x_in, coords, w, out):
     nc = tc.nc
     with ExitStack() as ctx:
         consts = ctx.enter_context(tc.tile_pool(name="consts", bufs=1))
-        raw_pool = ctx.enter_context(tc.tile_pool(name="raw", bufs=UNITS_AHEAD + 2))
+        raw_pool = ctx.enter_context(tc.tile_pool(name="raw", bufs=UNITS_AHEAD + 1))
         ordered_pool = ctx.enter_context(tc.tile_pool(name="ordered", bufs=REORDER_AHEAD + 1))
-        grouped_pool = ctx.enter_context(tc.tile_pool(name="grouped", bufs=3))
-        w_mx_pool = ctx.enter_context(tc.tile_pool(name="w_mx", bufs=QUARTERS + MX_LAG + 2))
+        grouped_pool = ctx.enter_context(tc.tile_pool(name="grouped", bufs=4))
+        w_mx_pool = ctx.enter_context(tc.tile_pool(name="w_mx", bufs=MX_LAG + 2))
         rope_pool = ctx.enter_context(tc.tile_pool(name="rope", bufs=2))
         bank_pool = ctx.enter_context(tc.psum_pool(name="banks", bufs=TRANSPOSE_BANKS))
         sum_pool = ctx.enter_context(tc.psum_pool(name="sums", bufs=2))
@@ -197,16 +196,12 @@ def tile_crossattnrope_pa_k_kernel(tc, x_in, coords, w, out):
         ordered_tiles = {}
 
         def reorder(n):
-            if n > last_unit or units[n][0] == "x":
+            if n > last_unit or units[n][0] == "x" or units[n][1] in STRIDED_QUARTERS:
                 return
             ordered = ordered_pool.tile([P, ROW_TILES * K_UNIT], BF16)
             src = raw_tiles[n][:].bitcast(F32).rearrange("q (n p u) -> q n u p", u=2, p=P)
             dst = ordered[:].bitcast(F32).rearrange("q (n u p) -> q n u p", u=2, p=P)
-            if units[n][1] in SPLIT_QUARTERS:
-                nc.vector.tensor_copy(out=dst[:, :PASSES_UNIT], in_=src[:, :PASSES_UNIT])
-                nc.scalar.copy(out=dst[:, PASSES_UNIT:], in_=src[:, PASSES_UNIT:])
-            else:
-                nc.vector.tensor_copy(out=dst, in_=src)
+            nc.vector.tensor_copy(out=dst, in_=src)
             ordered_tiles[n] = ordered
 
         grouped_tiles = {}
@@ -232,10 +227,7 @@ def tile_crossattnrope_pa_k_kernel(tc, x_in, coords, w, out):
                 dst = grouped_words[:, g * BANK : (g + 1) * BANK].rearrange(
                     "p (j r u) -> p j r u", j=ROW_TILES, u=2
                 )
-                if (n, g) in VECTOR_BANKS:
-                    nc.vector.tensor_copy(out=dst, in_=src)
-                else:
-                    nc.scalar.copy(out=dst, in_=src)
+                nc.scalar.copy(out=dst, in_=src)
 
         mx_tiles = {}
 
@@ -320,16 +312,17 @@ def tile_crossattnrope_pa_k_kernel(tc, x_in, coords, w, out):
             reorder(n)
         for n in range(last_unit + 1):
             load(n + UNITS_AHEAD)
-            reorder(n + REORDER_AHEAD)
             transpose(n)
             multiply_unit(n - MX_LAG)
             finish_group(n - MX_LAG - 1)
             if n > 0:
                 quantise(n - 1)
+            reorder(n + REORDER_AHEAD)
             if n == 4:
                 fill_tables(y, z)
 
-        multiply_unit(last_unit - 1)
+        for n in range(last_unit + 1 - MX_LAG, last_unit):
+            multiply_unit(n)
         quantise(last_unit)
         for b in range(BATCHES):
             multiply(GROUPS - 1, b, (QUARTERS - 1,))

@@ -36,7 +36,8 @@ TABLE_BLOCKS = BLOCKS_GROUP + AXES - 1
 
 UNITS_AHEAD = 10
 REORDER_AHEAD = 2
-MX_LAG = 3
+MX_RUN = 2
+MX_LAG = 2
 TRANSPOSE_BANKS = 6
 STRIDED_QUARTERS = (3,)
 
@@ -124,7 +125,7 @@ def tile_crossattnrope_pa_k_kernel(tc, x_in, coords, w, out):
         raw_pool = ctx.enter_context(tc.tile_pool(name="raw", bufs=UNITS_AHEAD + 1))
         ordered_pool = ctx.enter_context(tc.tile_pool(name="ordered", bufs=REORDER_AHEAD + 1))
         grouped_pool = ctx.enter_context(tc.tile_pool(name="grouped", bufs=4))
-        w_mx_pool = ctx.enter_context(tc.tile_pool(name="w_mx", bufs=MX_LAG + 2))
+        w_mx_pool = ctx.enter_context(tc.tile_pool(name="w_mx", bufs=MX_LAG + MX_RUN + 2))
         rope_pool = ctx.enter_context(tc.tile_pool(name="rope", bufs=2))
         bank_pool = ctx.enter_context(tc.psum_pool(name="banks", bufs=TRANSPOSE_BANKS))
         sum_pool = ctx.enter_context(tc.psum_pool(name="sums", bufs=2))
@@ -313,7 +314,9 @@ def tile_crossattnrope_pa_k_kernel(tc, x_in, coords, w, out):
         for n in range(last_unit + 1):
             load(n + UNITS_AHEAD)
             transpose(n)
-            multiply_unit(n - MX_LAG)
+            if n % MX_RUN == MX_RUN - 1:
+                for m in range(n - MX_LAG - MX_RUN + 1, n - MX_LAG + 1):
+                    multiply_unit(m)
             finish_group(n - MX_LAG - 1)
             if n > 0:
                 quantise(n - 1)

@@ -39,7 +39,8 @@ REORDER_AHEAD = 2
 MX_RUN = 2
 MX_LAG = 2
 TRANSPOSE_BANKS = 6
-STRIDED_QUARTERS = (3,)
+STRIDED_QUARTERS = (0,)
+RUN = 8
 
 FLOPS = 2 * BATCHES * TOKENS * FEATURES * K
 
@@ -197,11 +198,11 @@ def tile_crossattnrope_pa_k_kernel(tc, x_in, coords, w, out):
         ordered_tiles = {}
 
         def reorder(n):
-            if n > last_unit or units[n][0] == "x" or units[n][1] in STRIDED_QUARTERS:
+            if n > last_unit or units[n][1] in STRIDED_QUARTERS:
                 return
             ordered = ordered_pool.tile([P, ROW_TILES * K_UNIT], BF16)
-            src = raw_tiles[n][:].bitcast(F32).rearrange("q (n p u) -> q n u p", u=2, p=P)
-            dst = ordered[:].bitcast(F32).rearrange("q (n u p) -> q n u p", u=2, p=P)
+            src = raw_tiles[n][:].bitcast(F32).rearrange("r (n q u i) -> r n u q i", u=2, q=P // RUN, i=RUN)
+            dst = ordered[:].bitcast(F32).rearrange("r (n u q i) -> r n u q i", u=2, q=P // RUN, i=RUN)
             nc.vector.tensor_copy(out=dst, in_=src)
             ordered_tiles[n] = ordered
 

@@ -39,7 +39,9 @@ REORDER_AHEAD = 2
 MX_RUN = 2
 MX_LAG = 2
 TRANSPOSE_BANKS = 6
-STRIDED_QUARTERS = (0,)
+STEPPED_QUARTER = 0
+UNCOPIED = ("x", 0, 2, 4)
+SHARED_QUARTER = 1
 RUN = 8
 
 FLOPS = 2 * BATCHES * TOKENS * FEATURES * K
@@ -174,8 +176,7 @@ def tile_crossattnrope_pa_k_kernel(tc, x_in, coords, w, out):
         make_identity(nc, identity[:])
         freq_head, freq_tail = build_frequencies(nc, consts)
 
-        cos_table = consts.tile([P, BATCHES, TABLE_BLOCKS, 2, PAIRS], F32)
-        sin_table = consts.tile([P, BATCHES, TABLE_BLOCKS, 2, PAIRS], F32)
+        tables = consts.tile([P, BATCHES, 2, TABLE_BLOCKS, 2, PAIRS], F32)
 
         x_codes = consts.tile([P, QUARTERS * UNIT_WORDS], U32, align_bytes=64)
         x_scales = consts.tile([P, QUARTERS * UNIT_WORDS], U8, align_bytes=64)
@@ -188,22 +189,34 @@ def tile_crossattnrope_pa_k_kernel(tc, x_in, coords, w, out):
                 for first in range(0, TABLE_BLOCKS, AXES):
                     n = min(AXES, TABLE_BLOCKS - first)
                     nc.scalar.activation(
-                        out=sin_table[:, :, first : first + n, s, :], in_=y_axes[:, :, :n, :], func=ACT.Sin,
-                        scale=(-1.0 if s == 0 else 1.0),
+                        out=tables[:, :, 1, first : first + n, s, :], in_=y_axes[:, :, :n, :], func=ACT.Sin,
+                        scale=(1.0 if s == 0 else -1.0),
                     )
                     nc.scalar.activation(
-                        out=cos_table[:, :, first : first + n, s, :], in_=z_axes[:, :, :n, :], func=ACT.Sin
+                        out=tables[:, :, 0, first : first + n, s, :], in_=z_axes[:, :, :n, :], func=ACT.Sin
                     )
 
         ordered_tiles = {}
 
         def reorder(n):
-            if n > last_unit or units[n][1] in STRIDED_QUARTERS:
+            if n > last_unit:
                 return
+            owner, quarter = units[n]
+            src_order, dst_order = "r (n q u i) -> r n u q i", "r (n u q i) -> r n u q i"
+            sizes = {"u": 2, "q": P // RUN, "i": RUN}
+            if quarter == STEPPED_QUARTER:
+                if owner in UNCOPIED:
+                    return
+                src_order, dst_order = "r (n p u) -> r n u p", "r (n u p) -> r n u p"
+                sizes = {"u": 2, "p": P}
             ordered = ordered_pool.tile([P, ROW_TILES * K_UNIT], BF16)
-            src = raw_tiles[n][:].bitcast(F32).rearrange("r (n q u i) -> r n u q i", u=2, q=P // RUN, i=RUN)
-            dst = ordered[:].bitcast(F32).rearrange("r (n u q i) -> r n u q i", u=2, q=P // RUN, i=RUN)
-            nc.vector.tensor_copy(out=dst, in_=src)
+            src = raw_tiles[n][:].bitcast(F32).rearrange(src_order, **sizes)
+            dst = ordered[:].bitcast(F32).rearrange(dst_order, **sizes)
+            if quarter == SHARED_QUARTER and owner not in ("x", 0):
+                nc.vector.tensor_copy(out=dst[:, :PASSES_UNIT], in_=src[:, :PASSES_UNIT])
+                nc.scalar.copy(out=dst[:, PASSES_UNIT:], in_=src[:, PASSES_UNIT:])
+            else:
+                nc.vector.tensor_copy(out=dst, in_=src)
             ordered_tiles[n] = ordered
 
         grouped_tiles = {}
@@ -270,31 +283,34 @@ def tile_crossattnrope_pa_k_kernel(tc, x_in, coords, w, out):
                         stop=(quarter == QUARTERS - 1 and g == PASSES_UNIT - 1),
                     )
 
-        def rotate_and_store(group, b):
+        def rotate_and_store(group, batches):
             cols = slice(group * ROWS, (group + 1) * ROWS)
             axis = group * BLOCKS_GROUP % AXES
             blocks = slice(axis, axis + BLOCKS_GROUP)
-            total = sums[(group, b)]
-            turned = rotated[:, b, cols]
-            crossed = rope_pool.tile([P, ROWS], F32)
+            products = rope_pool.tile([P, BATCHES, 2, ROWS], F32)
+            for b in batches:
+                nc.vector.tensor_tensor(
+                    out=products[:, b],
+                    in0=sums[(group, b)][:].unsqueeze(1).to_broadcast([P, 2, ROWS]),
+                    in1=tables[:, b, :, blocks].rearrange("p t c s i -> p t (c s i)"),
+                    op=ALU.mult,
+                )
             halves = "p (c s i) -> p c s i"
-            nc.vector.tensor_tensor(
-                out=turned, in0=total[:], in1=cos_table[:, b, blocks].rearrange("p c s i -> p (c s i)"), op=ALU.mult
-            )
-            nc.vector.tensor_tensor(
-                out=crossed[:].rearrange(halves, s=2, i=PAIRS),
-                in0=total[:].rearrange(halves, s=2, i=PAIRS)[:, :, ::-1, :],
-                in1=sin_table[:, b, blocks],
-                op=ALU.mult,
-            )
-            nc.vector.tensor_tensor(out=turned, in0=turned, in1=crossed[:], op=ALU.add)
+            for b in batches:
+                nc.vector.tensor_tensor(
+                    out=rotated[:, b, cols].rearrange(halves, s=2, i=PAIRS),
+                    in0=products[:, b, 0].rearrange(halves, s=2, i=PAIRS),
+                    in1=products[:, b, 1].rearrange(halves, s=2, i=PAIRS)[:, :, ::-1, :],
+                    op=ALU.add,
+                )
             first_head, end_head = group * ROWS // HEAD_DIM, (group + 1) * ROWS // HEAD_DIM
-            nc.sync.dma_start(
-                out=out[b, first_head:end_head].rearrange("h l d -> l h d"),
-                in_=rotated[:, b, first_head * HEAD_DIM : end_head * HEAD_DIM].rearrange(
-                    "p (h d) -> p h d", d=HEAD_DIM
-                ),
-            )
+            for b in batches:
+                nc.sync.dma_start(
+                    out=out[b, first_head:end_head].rearrange("h l d -> l h d"),
+                    in_=rotated[:, b, first_head * HEAD_DIM : end_head * HEAD_DIM].rearrange(
+                        "p (h d) -> p h d", d=HEAD_DIM
+                    ),
+                )
 
         def multiply_unit(n):
             if n < 0 or units[n][0] == "x":
@@ -306,8 +322,7 @@ def tile_crossattnrope_pa_k_kernel(tc, x_in, coords, w, out):
         def finish_group(n):
             if n < 0 or units[n][0] == "x" or units[n][1] < QUARTERS - 1:
                 return
-            for b in range(BATCHES):
-                rotate_and_store(units[n][0], b)
+            rotate_and_store(units[n][0], range(BATCHES))
 
         y, z = build_angles(nc, consts, coords_bf, freq_head, freq_tail)
         for n in range(REORDER_AHEAD):
@@ -322,7 +337,7 @@ def tile_crossattnrope_pa_k_kernel(tc, x_in, coords, w, out):
             if n > 0:
                 quantise(n - 1)
             reorder(n + REORDER_AHEAD)
-            if n == 4:
+            if n == 0:
                 fill_tables(y, z)
 
         for n in range(last_unit + 1 - MX_LAG, last_unit):
@@ -330,4 +345,4 @@ def tile_crossattnrope_pa_k_kernel(tc, x_in, coords, w, out):
         quantise(last_unit)
         for b in range(BATCHES):
             multiply(GROUPS - 1, b, (QUARTERS - 1,))
-            rotate_and_store(GROUPS - 1, b)
+            rotate_and_store(GROUPS - 1, (b,))

from contextlib import ExitStack
import math

import concourse.mybir as mybir
from concourse.masks import make_identity

F32 = mybir.dt.float32
BF16 = mybir.dt.bfloat16
U32 = mybir.dt.uint32
U8 = mybir.dt.uint8
FP8X4 = mybir.dt.float8_e4m3fn_x4
ALU = mybir.AluOpType
ACT = mybir.ActivationFunctionType

P = 128
BATCHES, TOKENS, K = 2, 128, 8192
HEADS, HEAD_DIM, AXES, PAIRS = 16, 96, 3, 16
FEATURES = HEADS * HEAD_DIM
ROPE_BASE = 10000.0

K_PASS = 512
PASS_WORDS = K_PASS // 2
ROWS = 256
ROW_TILES = ROWS // P
PASSES_UNIT = 4
K_UNIT = PASSES_UNIT * K_PASS
QUARTERS = K // K_UNIT
GROUPS = FEATURES // ROWS
BANK = 512
UNIT_WORDS = PASSES_UNIT * ROWS
PAIR_WORDS = 2 * ROWS

BLOCK = 2 * PAIRS
BLOCKS_GROUP = ROWS // BLOCK
TABLE_BLOCKS = BLOCKS_GROUP + AXES - 1

UNITS_AHEAD = 10
REORDER_AHEAD = 2
MX_RUN = 2
MX_LAG = 2
TRANSPOSE_BANKS = 6
STEPPED_QUARTER = 0
UNCOPIED = ("x", 0, 2, 4)
SHARED_QUARTER = 1
RUN = 8

FLOPS = 2 * BATCHES * TOKENS * FEATURES * K

ROUND_MAGIC = 1.5 * 2.0**23


def leading_bits(value, bits):
    scale = 1.0
    while abs(value) * scale < 2.0 ** (bits - 1):
        scale *= 2.0
    while abs(value) * scale >= 2.0**bits:
        scale /= 2.0
    return round(value * scale) / scale


def build_frequencies(nc, consts):
    freq_head = consts.tile([P, PAIRS], F32)
    freq_tail = consts.tile([P, PAIRS], F32)
    for i in range(PAIRS):
        inv_freq = ROPE_BASE ** (-i / PAIRS)
        head = leading_bits(inv_freq, 24)
        nc.gpsimd.memset(freq_head[:, i : i + 1], head)
        nc.gpsimd.memset(freq_tail[:, i : i + 1], inv_freq - head)
    return freq_head, freq_tail


def build_angles(nc, consts, coords_bf, freq_head, freq_tail):
    columns = BATCHES * AXES
    shape = [P, columns, PAIRS]

    coords_f = consts.tile([P, columns], F32)
    nc.vector.tensor_copy(out=coords_f[:], in_=coords_bf[:].rearrange("p b a -> p (b a)"))

    coords_wide = coords_f[:].unsqueeze(2).to_broadcast(shape)
    angle = consts.tile(shape, F32)
    angle_tail = consts.tile(shape, F32)
    nc.vector.tensor_tensor(
        out=angle[:], in0=coords_wide, in1=freq_head[:].unsqueeze(1).to_broadcast(shape), op=ALU.mult
    )
    nc.vector.tensor_tensor(
        out=angle_tail[:], in0=coords_wide, in1=freq_tail[:].unsqueeze(1).to_broadcast(shape), op=ALU.mult
    )
    nc.vector.tensor_tensor(out=angle[:], in0=angle[:], in1=angle_tail[:], op=ALU.add)

    turns = consts.tile(shape, F32)
    nc.vector.tensor_scalar(
        out=turns[:], in0=angle[:], scalar1=1.0 / (2.0 * math.pi), scalar2=ROUND_MAGIC, op0=ALU.mult, op1=ALU.add
    )
    nc.vector.tensor_scalar(out=turns[:], in0=turns[:], scalar1=ROUND_MAGIC, scalar2=None, op0=ALU.subtract)

    y = consts.tile(shape, F32)
    part1 = leading_bits(2.0 * math.pi, 12)
    part2 = leading_bits(2.0 * math.pi - part1, 12)
    part3 = 2.0 * math.pi - part1 - part2
    flat = "p c i -> p (c i)"
    nc.vector.scalar_tensor_tensor(
        out=y[:].rearrange(flat), in0=turns[:].rearrange(flat), scalar=-part1, in1=angle[:].rearrange(flat),
        op0=ALU.mult, op1=ALU.add,
    )
    for part in (part2, part3):
        nc.vector.scalar_tensor_tensor(
            out=y[:].rearrange(flat), in0=turns[:].rearrange(flat), scalar=-part, in1=y[:].rearrange(flat),
            op0=ALU.mult, op1=ALU.add,
        )
    pi_below = int(math.pi * 2.0**22) / 2.0**22
    nc.vector.tensor_scalar(out=y[:], in0=y[:], scalar1=pi_below, scalar2=-pi_below, op0=ALU.min, op1=ALU.max)

    z = consts.tile(shape, F32)
    half_pi_head = leading_bits(math.pi / 2.0, 24)
    nc.vector.scalar_tensor_tensor(
        out=z[:].rearrange(flat), in0=y[:].rearrange(flat), scalar=-1.0, in1=y[:].rearrange(flat),
        op0=ALU.mult, op1=ALU.max,
    )
    nc.vector.tensor_scalar(out=z[:], in0=z[:], scalar1=-1.0, scalar2=half_pi_head, op0=ALU.mult, op1=ALU.add)
    nc.vector.tensor_scalar(out=z[:], in0=z[:], scalar1=math.pi / 2.0 - half_pi_head, scalar2=None, op0=ALU.add)
    return y, z


def tile_crossattnrope_pa_k_kernel(tc, x_in, coords, w, out):
    nc = tc.nc
    with ExitStack() as ctx:
        consts = ctx.enter_context(tc.tile_pool(name="consts", bufs=1))
        raw_pool = ctx.enter_context(tc.tile_pool(name="raw", bufs=UNITS_AHEAD + 1))
        ordered_pool = ctx.enter_context(tc.tile_pool(name="ordered", bufs=REORDER_AHEAD + 1))
        grouped_pool = ctx.enter_context(tc.tile_pool(name="grouped", bufs=4))
        w_mx_pool = ctx.enter_context(tc.tile_pool(name="w_mx", bufs=MX_LAG + MX_RUN + 2))
        rope_pool = ctx.enter_context(tc.tile_pool(name="rope", bufs=2))
        bank_pool = ctx.enter_context(tc.psum_pool(name="banks", bufs=TRANSPOSE_BANKS))
        sum_pool = ctx.enter_context(tc.psum_pool(name="sums", bufs=2))
        ctx.enter_context(tc.manual_schedule())

        x_rows = x_in.rearrange("b l k -> l b k")
        units = []
        for quarter in range(QUARTERS):
            units.extend([("x", quarter), (0, quarter)])
        units.extend((group, quarter) for group in range(1, GROUPS) for quarter in range(QUARTERS))
        last_unit = len(units) - 1

        raw_tiles = []

        def load(n):
            if n > last_unit:
                return
            owner, quarter = units[n]
            raw = raw_pool.tile([P, ROW_TILES * K_UNIT], BF16)
            pieces = PASSES_UNIT if n == 0 else 1
            width = K_UNIT // pieces
            for c in range(pieces):
                first_k = quarter * K_UNIT + c * width
                k_cols = slice(first_k, first_k + width)
                if owner == "x":
                    rows = x_rows[:, :, k_cols]
                else:
                    rows = w[owner * ROWS : (owner + 1) * ROWS, k_cols].rearrange("(j p) k -> p j k", p=P)
                nc.sync.dma_start(
                    out=raw[:].rearrange("p (j k) -> p j k", j=ROW_TILES)[:, :, c * width : (c + 1) * width], in_=rows
                )
            raw_tiles.append(raw)

        coords_bf = consts.tile([P, BATCHES, AXES], BF16)
        nc.scalar.dma_start(out=coords_bf[:], in_=coords.rearrange("b l a -> l b a"))
        for n in range(UNITS_AHEAD):
            load(n)

        zero = consts.tile([P, 1], F32)
        nc.vector.memset(zero[:], 0.0)
        warm = consts.tile([P, 1], F32)
        nc.scalar.activation(out=warm[:], in_=zero[:], func=ACT.Sin)

        identity = consts.tile([P, P], F32)
        make_identity(nc, identity[:])
        freq_head, freq_tail = build_frequencies(nc, consts)

        tables = consts.tile([P, BATCHES, 2, TABLE_BLOCKS, 2, PAIRS], F32)

        x_codes = consts.tile([P, QUARTERS * UNIT_WORDS], U32, align_bytes=64)
        x_scales = consts.tile([P, QUARTERS * UNIT_WORDS], U8, align_bytes=64)
        rotated = consts.tile([P, BATCHES, FEATURES], F32)

        def fill_tables(y, z):
            y_axes = y[:].rearrange("p (b a) i -> p b a i", b=BATCHES)
            z_axes = z[:].rearrange("p (b a) i -> p b a i", b=BATCHES)
            for s in range(2):
                for first in range(0, TABLE_BLOCKS, AXES):
                    n = min(AXES, TABLE_BLOCKS - first)
                    nc.scalar.activation(
                        out=tables[:, :, 1, first : first + n, s, :], in_=y_axes[:, :, :n, :], func=ACT.Sin,
                        scale=(1.0 if s == 0 else -1.0),
                    )
                    nc.scalar.activation(
                        out=tables[:, :, 0, first : first + n, s, :], in_=z_axes[:, :, :n, :], func=ACT.Sin
                    )

        ordered_tiles = {}

        def reorder(n):
            if n > last_unit:
                return
            owner, quarter = units[n]
            src_order, dst_order = "r (n q u i) -> r n u q i", "r (n u q i) -> r n u q i"
            sizes = {"u": 2, "q": P // RUN, "i": RUN}
            if quarter == STEPPED_QUARTER:
                if owner in UNCOPIED:
                    return
                src_order, dst_order = "r (n p u) -> r n u p", "r (n u p) -> r n u p"
                sizes = {"u": 2, "p": P}
            ordered = ordered_pool.tile([P, ROW_TILES * K_UNIT], BF16)
            src = raw_tiles[n][:].bitcast(F32).rearrange(src_order, **sizes)
            dst = ordered[:].bitcast(F32).rearrange(dst_order, **sizes)
            if quarter == SHARED_QUARTER and owner not in ("x", 0):
                nc.vector.tensor_copy(out=dst[:, :PASSES_UNIT], in_=src[:, :PASSES_UNIT])
                nc.scalar.copy(out=dst[:, PASSES_UNIT:], in_=src[:, PASSES_UNIT:])
            else:
                nc.vector.tensor_copy(out=dst, in_=src)
            ordered_tiles[n] = ordered

        grouped_tiles = {}

        def transpose(n):
            grouped = grouped_pool.tile([P, PASSES_UNIT * 4 * ROWS], BF16, align_bytes=64)
            grouped_tiles[n] = grouped
            grouped_words = grouped[:].bitcast(F32)
            for g in range(PASSES_UNIT):
                bank = bank_pool.tile([P, BANK], F32)
                for j in range(ROW_TILES):
                    first_word = (j * PASSES_UNIT + g) * PASS_WORDS
                    for u in range(2):
                        if n in ordered_tiles:
                            words = ordered_tiles[n][:].bitcast(F32)
                            piece = words[:, first_word + u * P : first_word + (u + 1) * P]
                        else:
                            words = raw_tiles[n][:].bitcast(F32)
                            piece = words[:, first_word + u : first_word + PASS_WORDS : 2]
                        column = (j * 2 + u) * P
                        nc.tensor.transpose(bank[:, column : column + P], piece, identity[:])
                src = bank[:].rearrange("p (j u r) -> p j r u", j=ROW_TILES, u=2)
                dst = grouped_words[:, g * BANK : (g + 1) * BANK].rearrange(
                    "p (j r u) -> p j r u", j=ROW_TILES, u=2
                )
                nc.scalar.copy(out=dst, in_=src)

        mx_tiles = {}

        def quantise(n):
            owner, quarter = units[n]
            if owner == "x":
                codes = x_codes[:, quarter * UNIT_WORDS : (quarter + 1) * UNIT_WORDS]
                scales = x_scales[:, quarter * UNIT_WORDS : (quarter + 1) * UNIT_WORDS]
            else:
                w_codes = w_mx_pool.tile([P, UNIT_WORDS], U32, align_bytes=64)
                w_scales = w_mx_pool.tile([P, UNIT_WORDS], U8, align_bytes=64)
                codes, scales = w_codes[:], w_scales[:]
                mx_tiles[(owner, quarter)] = (codes, scales)
            for first in range(0, UNIT_WORDS, PAIR_WORDS):
                nc.vector.quantize_mx(
                    out=codes[:, first : first + PAIR_WORDS].bitcast(FP8X4),
                    scales=scales[:, first : first + PAIR_WORDS],
                    in_=grouped_tiles[n][:, 4 * first : 4 * (first + PAIR_WORDS)],
                )

        sums = {}

        def multiply(group, b, quarters):
            if quarters[0] == 0:
                total = sum_pool.tile([P, ROWS], F32)
                sums[(group, b)] = total
            for quarter in quarters:
                codes, scales = mx_tiles[(group, quarter)]
                for g in range(PASSES_UNIT):
                    x_first = ((quarter * PASSES_UNIT + g) * BATCHES + b) * P
                    nc.tensor.matmul_mx(
                        out=sums[(group, b)][:],
                        lhsT=x_codes[:, x_first : x_first + P].bitcast(FP8X4),
                        lhsT_scale=x_scales[:, x_first : x_first + P],
                        rhs=codes[:, g * ROWS : (g + 1) * ROWS].bitcast(FP8X4),
                        rhs_scale=scales[:, g * ROWS : (g + 1) * ROWS],
                        start=(quarter == 0 and g == 0),
                        stop=(quarter == QUARTERS - 1 and g == PASSES_UNIT - 1),
                    )

        def rotate_and_store(group, batches):
            cols = slice(group * ROWS, (group + 1) * ROWS)
            axis = group * BLOCKS_GROUP % AXES
            blocks = slice(axis, axis + BLOCKS_GROUP)
            products = rope_pool.tile([P, BATCHES, 2, ROWS], F32)
            for b in batches:
                nc.vector.tensor_tensor(
                    out=products[:, b],
                    in0=sums[(group, b)][:].unsqueeze(1).to_broadcast([P, 2, ROWS]),
                    in1=tables[:, b, :, blocks].rearrange("p t c s i -> p t (c s i)"),
                    op=ALU.mult,
                )
            halves = "p (c s i) -> p c s i"
            for b in batches:
                nc.vector.tensor_tensor(
                    out=rotated[:, b, cols].rearrange(halves, s=2, i=PAIRS),
                    in0=products[:, b, 0].rearrange(halves, s=2, i=PAIRS),
                    in1=products[:, b, 1].rearrange(halves, s=2, i=PAIRS)[:, :, ::-1, :],
                    op=ALU.add,
                )
            first_head, end_head = group * ROWS // HEAD_DIM, (group + 1) * ROWS // HEAD_DIM
            for b in batches:
                nc.sync.dma_start(
                    out=out[b, first_head:end_head].rearrange("h l d -> l h d"),
                    in_=rotated[:, b, first_head * HEAD_DIM : end_head * HEAD_DIM].rearrange(
                        "p (h d) -> p h d", d=HEAD_DIM
                    ),
                )

        def multiply_unit(n):
            if n < 0 or units[n][0] == "x":
                return
            group, quarter = units[n]
            for b in range(BATCHES):
                multiply(group, b, (quarter,))

        def finish_group(n):
            if n < 0 or units[n][0] == "x" or units[n][1] < QUARTERS - 1:
                return
            rotate_and_store(units[n][0], range(BATCHES))

        y, z = build_angles(nc, consts, coords_bf, freq_head, freq_tail)
        for n in range(REORDER_AHEAD):
            reorder(n)
        for n in range(last_unit + 1):
            load(n + UNITS_AHEAD)
            transpose(n)
            if n % MX_RUN == MX_RUN - 1:
                for m in range(n - MX_LAG - MX_RUN + 1, n - MX_LAG + 1):
                    multiply_unit(m)
            finish_group(n - MX_LAG - 1)
            if n > 0:
                quantise(n - 1)
            reorder(n + REORDER_AHEAD)
            if n == 0:
                fill_tables(y, z)

        for n in range(last_unit + 1 - MX_LAG, last_unit):
            multiply_unit(n)
        quantise(last_unit)
        for b in range(BATCHES):
            multiply(GROUPS - 1, b, (QUARTERS - 1,))
            rotate_and_store(GROUPS - 1, (b,))
